import numpy as np
import ml_dtypes


def mxq(x, axis, fmt="e4m3"):
    dtype, down = {"e4m3": (ml_dtypes.float8_e4m3fn, 7), "e5m2": (ml_dtypes.float8_e5m2, 14)}[fmt]
    v = np.moveaxis(np.asarray(x, np.float32).astype(ml_dtypes.bfloat16).astype(np.float64), axis, -1)
    blocks = v.reshape(v.shape[:-1] + (-1, 32))
    amax = np.abs(blocks).max(-1, keepdims=True)
    byte = np.maximum(np.where(amax > 0, np.frexp(amax)[1] - 1 + 127, 0) - down, 1)
    scale = np.exp2(byte - 127.0)
    codes = (blocks / scale).astype(np.float32).astype(dtype).astype(np.float64)
    return np.moveaxis((codes * scale).reshape(v.shape), -1, axis)


WIDE = False


def mx_kscale(k):
    if not WIDE:
        return np.ones(k)
    levels = np.array([10, -10, 5, -5, 0])
    a = np.random.permutation(np.resize(levels, k // 512 * 4)).reshape(k // 512, 4)
    idx = np.arange(k)
    return np.exp2(a[idx // 512, idx % 128 // 32])


BF16 = ml_dtypes.bfloat16


def bf(x):
    return np.asarray(x, np.float32).astype(BF16)


def f64(x):
    return np.asarray(x).astype(np.float64)


T, B, D, U, V, E = 3, 4096, 512, 1024, 16, 8
G = 2 * E


def softmax(v):
    e = np.exp(v - v.max(-1, keepdims=True))
    return e / e.sum(-1, keepdims=True)


def setup_inputs():
    rn = np.random.standard_normal
    s = mx_kscale(U)
    return {
        "task_h": bf(np.abs(rn((T, B, U))) * 0.55 * s),
        "share_h": bf(np.abs(rn((B, U))) * 0.5 * s),
        "ews1": bf(rn((U, V, E)) * 2.0 / np.sqrt(U) / s[:, None, None]),
        "ebs1": bf(rn((V, E)) * 0.5),
        "ew1": bf(rn((T, U, V, E)) * 2.0 / np.sqrt(U) / s[None, :, None, None]),
        "eb1": bf(rn((T, V, E)) * 0.5),
        "gate_pre1": bf(rn((T, B, G))),
        "gb1": bf(rn((T, G)) * 0.5),
    }


def reference(task_h, share_h, ews1, ebs1, ew1, eb1, gate_pre1, gb1):
    es = np.maximum((mxq(f64(share_h), 1, "e4m3") @ mxq(f64(ews1).reshape(U, V * E), 0, "e4m3")).reshape(B, V, E) + f64(ebs1), 0.0)
    et = np.maximum((mxq(f64(task_h), 2, "e4m3") @ mxq(f64(ew1).reshape(T, U, V * E), 1, "e4m3")).reshape(T, B, V, E) + f64(eb1)[:, None], 0.0)
    g = softmax(f64(gate_pre1) + f64(gb1)[:, None])
    comb = np.concatenate([et, np.broadcast_to(es, et.shape)], axis=-1)
    return (comb * g[:, :, None, :]).sum(-1)

@@ -1,0 +1,223 @@
+from contextlib import ExitStack
+
+import concourse.mybir as mybir
+from concourse.masks import make_identity
+
+F32 = mybir.dt.float32
+BF16 = mybir.dt.bfloat16
+U32 = mybir.dt.uint32
+U8 = mybir.dt.uint8
+FP8X4 = mybir.dt.float8_e4m3fn_x4
+ACT = mybir.ActivationFunctionType
+ALU = mybir.AluOpType
+AX = mybir.AxisListType
+
+P = 128
+T, B, U, V, E = 3, 4096, 1024, 16, 8
+G = 2 * E
+C = V * E
+STREAMS = T + 1
+PACK = 4
+K_PASS = P * PACK
+PASSES = U // K_PASS
+ROWS = B // P
+J = 4
+N = J * P
+CHUNKS = ROWS // J
+UNITS = CHUNKS * STREAMS
+WORDS = U // 2
+AHEAD = 5
+
+FLOPS = 2 * STREAMS * B * U * C
+
+
+def tile_plelayer_pb_t_kernel(tc, task_h, share_h, ews1, ebs1, ew1, eb1, gate_pre1, gb1, out):
+    nc = tc.nc
+    stream_rows = [share_h.rearrange("(p j) u -> p (j u)", p=P)]
+    stream_rows += [task_h[t].rearrange("(p j) u -> p (j u)", p=P) for t in range(T)]
+    out_rows = out.rearrange("t (p j) v -> p t (j v)", p=P)
+
+    with ExitStack() as ctx:
+        const = ctx.enter_context(tc.tile_pool(name="const", bufs=1))
+        x_pool = ctx.enter_context(tc.tile_pool(name="x", bufs=AHEAD + 1))
+        mx_pool = ctx.enter_context(tc.tile_pool(name="mx", bufs=3))
+        prod_pool = ctx.enter_context(tc.tile_pool(name="prod", bufs=2 * T))
+        fwd_ps = ctx.enter_context(tc.psum_pool(name="fwd", bufs=4))
+        acc_ps = ctx.enter_context(tc.psum_pool(name="acc", bufs=2))
+        nat_ps = ctx.enter_context(tc.psum_pool(name="nat", bufs=2))
+        ctx.enter_context(tc.manual_schedule())
+
+        x_tiles, grouped_tiles, code_tiles, scale_tiles = {}, {}, {}, {}
+        acc_tiles, relu_tiles, nat_tiles, prod_tiles = {}, {}, {}, {}
+
+        def load(n):
+            chunk, stream = divmod(n, STREAMS)
+            x_tiles[n] = x_pool.tile([P, J * U], BF16, name="x_rows")
+            nc.sync.dma_start(out=x_tiles[n][:], in_=stream_rows[stream][:, chunk * J * U : (chunk + 1) * J * U])
+
+        ident = const.tile([P, P], F32)
+        make_identity(nc, ident[:])
+        bias_rows = const.tile([P, P], BF16)
+        nc.vector.memset(bias_rows[:], 0.0)
+
+        gate_raw = const.tile([P, T * ROWS * G], BF16)
+        nc.sync.dma_start(
+            out=gate_raw[:].rearrange("p (t r) -> p t r", t=T),
+            in_=gate_pre1.rearrange("t (p j) g -> p t (j g)", p=P),
+        )
+        for n in range(AHEAD):
+            load(n)
+        gb_rep = const.tile([P, T * G], BF16)
+        nc.scalar.dma_start(out=gb_rep[:], in_=gb1.rearrange("t g -> (t g)").partition_broadcast(P))
+        nc.scalar.dma_start(out=bias_rows[0:1, :], in_=ebs1.rearrange("v x -> (v x)").unsqueeze(0))
+        nc.scalar.dma_start(out=bias_rows[1:STREAMS, :], in_=eb1.rearrange("t v x -> t (v x)"))
+        w_raw = const.tile([P, STREAMS, PASSES, PACK, C], BF16)
+        nc.scalar.dma_start(
+            out=w_raw[:, 0].rearrange("q g t c -> q (g t c)").rearrange("q (a r) -> q a r", a=4),
+            in_=ews1.rearrange("(a q e) v x -> q a (e v x)", a=4, q=P, e=2),
+        )
+        nc.scalar.dma_start(
+            out=w_raw[:, 1:STREAMS].rearrange("q s g t c -> q s (g t c)").rearrange("q s (a r) -> q s a r", a=4),
+            in_=ew1.rearrange("s (a q e) v x -> q s a (e v x)", a=4, q=P, e=2),
+        )
+
+        gate = const.tile([P, T * ROWS, G], F32)
+        nc.vector.tensor_tensor(
+            out=gate[:].rearrange("p (t j) g -> p t j g", t=T),
+            in0=gate_raw[:].rearrange("p (t j g) -> p t j g", t=T, j=ROWS),
+            in1=gb_rep[:].rearrange("p (t g) -> p t g", t=T).unsqueeze(2).to_broadcast([P, T, ROWS, G]),
+            op=ALU.add,
+        )
+        gate_max = const.tile([P, T * ROWS], F32)
+        nc.vector.tensor_reduce(out=gate_max[:], in_=gate[:], axis=AX.X, op=ALU.max)
+        nc.vector.tensor_tensor(
+            out=gate[:],
+            in0=gate[:],
+            in1=gate_max[:].unsqueeze(2).to_broadcast([P, T * ROWS, G]),
+            op=ALU.subtract,
+        )
+
+        bias_rows_f32 = const.tile([P, P], F32)
+        nc.vector.tensor_copy(out=bias_rows_f32[:], in_=bias_rows[:])
+
+        w_grouped = const.tile([P, STREAMS, PASSES, C, PACK], BF16, align_bytes=64)
+        w_codes = const.tile([P, STREAMS, PASSES, C], U32, align_bytes=64)
+        w_scales = const.tile([P, STREAMS, PASSES, C], U8, align_bytes=64)
+        for s in range(STREAMS):
+            nc.vector.tensor_copy(out=w_grouped[:, s], in_=w_raw[:, s].rearrange("q g t c -> q g c t"))
+        for s in range(STREAMS):
+            nc.vector.quantize_mx(
+                out=w_codes[:, s].rearrange("q g c -> q (g c)").bitcast(FP8X4),
+                scales=w_scales[:, s].rearrange("q g c -> q (g c)"),
+                in_=w_grouped[:, s].rearrange("q g c t -> q (g c t)"),
+            )
+
+        def transpose_in(n):
+            x_words = x_tiles[n][:].bitcast(F32)
+            grouped_tiles[n] = mx_pool.tile([P, PASSES * N * PACK], BF16, name="grouped", align_bytes=64)
+            grouped_words = grouped_tiles[n][:].bitcast(F32).rearrange("q (g c h) -> q g c h", g=PASSES, h=2)
+            for j in range(J):
+                xt = fwd_ps.tile([P, 4, P], F32, name="xt")
+                for a in range(4):
+                    nc.tensor.transpose(xt[:, a, :], x_words[:, j * WORDS + a * P : j * WORDS + (a + 1) * P], ident[:])
+                nc.scalar.copy(
+                    out=grouped_words[:, :, j * P : (j + 1) * P, :],
+                    in_=xt[:].rearrange("q (g h) r -> q g r h", g=PASSES),
+                )
+
+        def quantise(n):
+            code_tiles[n] = mx_pool.tile([P, PASSES * N], U32, name="codes", align_bytes=64)
+            scale_tiles[n] = mx_pool.tile([P, PASSES * N], U8, name="scales", align_bytes=64)
+            nc.vector.quantize_mx(
+                out=code_tiles[n][:].bitcast(FP8X4), scales=scale_tiles[n][:], in_=grouped_tiles[n][:]
+            )
+
+        def expert_matmul(n):
+            s = n % STREAMS
+            acc_tiles[n] = acc_ps.tile([P, N], F32, name="acc")
+            for g in range(PASSES):
+                nc.tensor.matmul_mx(
+                    out=acc_tiles[n][:],
+                    lhsT=w_codes[:, s, g, :].bitcast(FP8X4),
+                    lhsT_scale=w_scales[:, s, g, :],
+                    rhs=code_tiles[n][:, g * N : (g + 1) * N].bitcast(FP8X4),
+                    rhs_scale=scale_tiles[n][:, g * N : (g + 1) * N],
+                    start=(g == 0),
+                    stop=(g == PASSES - 1),
+                )
+
+        def bias_relu(n):
+            s = n % STREAMS
+            relu_tiles[n] = mx_pool.tile([P, N], F32, name="relu")
+            nc.scalar.activation(
+                out=relu_tiles[n][:], in_=acc_tiles[n][:], func=ACT.Relu, bias=bias_col[:, s : s + 1], scale=1.0
+            )
+
+        def transpose_back(n):
+            nat_tiles[n] = nat_ps.tile([P, J, C], F32, name="nat")
+            for j in range(J):
+                nc.tensor.transpose(nat_tiles[n][:, j, :], relu_tiles[n][:, j * P : (j + 1) * P], ident[:])
+
+        def weigh(n, t, half):
+            chunk = n // STREAMS
+            rows = slice(t * ROWS + chunk * J, t * ROWS + (chunk + 1) * J)
+            nc.vector.tensor_tensor(
+                out=prod_tiles[(chunk, t)][:, :, :, half * E : (half + 1) * E],
+                in0=nat_tiles[n][:].rearrange("p j (v e) -> p j v e", v=V),
+                in1=gate[:, rows, half * E : (half + 1) * E].unsqueeze(2).to_broadcast([P, J, V, E]),
+                op=ALU.mult,
+            )
+
+        def gate_and_sum(n):
+            chunk, s = divmod(n, STREAMS)
+            if s == 0:
+                for t in range(T):
+                    prod_tiles[(chunk, t)] = prod_pool.tile([P, J, V, G], F32, name="prod")
+                    weigh(n, t, 1)
+            else:
+                t = s - 1
+                weigh(n, t, 0)
+                nc.vector.tensor_reduce(
+                    out=out_sb[:, t, chunk * J * V : (chunk + 1) * J * V],
+                    in_=prod_tiles[(chunk, t)][:].rearrange("p j v g -> p (j v) g"),
+                    axis=AX.X,
+                    op=ALU.add,
+                )
+            if s == T:
+                cols = slice(chunk * J * V, (chunk + 1) * J * V)
+                nc.sync.dma_start(out=out_rows[:, :, cols], in_=out_sb[:, :, cols])
+
+        out_sb = const.tile([P, T, ROWS * V], F32)
+
+        transpose_in(0)
+
+        bias_ps = nat_ps.tile([P, J, C], F32, name="nat")
+        nc.tensor.transpose(bias_ps[:, 0, :], bias_rows_f32[:], ident[:])
+        bias_col = const.tile([P, STREAMS], F32)
+        nc.vector.tensor_copy(out=bias_col[:], in_=bias_ps[:, 0, 0:STREAMS])
+
+        nc.scalar.activation(out=gate[:], in_=gate[:], func=ACT.Exp)
+        gate_sum = const.tile([P, T * ROWS], F32)
+        nc.vector.tensor_reduce(out=gate_sum[:], in_=gate[:], axis=AX.X, op=ALU.add)
+        nc.vector.reciprocal(out=gate_sum[:], in_=gate_sum[:])
+        nc.vector.tensor_tensor(
+            out=gate[:],
+            in0=gate[:],
+            in1=gate_sum[:].unsqueeze(2).to_broadcast([P, T * ROWS, G]),
+            op=ALU.mult,
+        )
+
+        for step in range(1, UNITS + 3):
+            if step + AHEAD - 1 < UNITS:
+                load(step + AHEAD - 1)
+            if step - 1 < UNITS:
+                quantise(step - 1)
+            if 0 <= step - 2 < UNITS:
+                expert_matmul(step - 2)
+                bias_relu(step - 2)
+            if step < UNITS:
+                transpose_in(step)
+            if 0 <= step - 2 < UNITS:
+                transpose_back(step - 2)
+            if 0 <= step - 3:
+                gate_and_sum(step - 3)

@@ -41,14 +41,14 @@ def tile_plelayer_pb_t_kernel(tc, task_h, share_h, ews1, ebs1, ew1, eb1, gate_pr
         const = ctx.enter_context(tc.tile_pool(name="const", bufs=1))
         x_pool = ctx.enter_context(tc.tile_pool(name="x", bufs=AHEAD + 1))
         mx_pool = ctx.enter_context(tc.tile_pool(name="mx", bufs=3))
-        prod_pool = ctx.enter_context(tc.tile_pool(name="prod", bufs=2 * T))
+        shared_pool = ctx.enter_context(tc.tile_pool(name="shared", bufs=2 * T))
         fwd_ps = ctx.enter_context(tc.psum_pool(name="fwd", bufs=4))
         acc_ps = ctx.enter_context(tc.psum_pool(name="acc", bufs=2))
         nat_ps = ctx.enter_context(tc.psum_pool(name="nat", bufs=2))
         ctx.enter_context(tc.manual_schedule())
 
         x_tiles, grouped_tiles, code_tiles, scale_tiles = {}, {}, {}, {}
-        acc_tiles, relu_tiles, nat_tiles, prod_tiles = {}, {}, {}, {}
+        acc_tiles, relu_tiles, nat_tiles, sum_tiles = {}, {}, {}, {}
 
         def load(n):
             chunk, stream = divmod(n, STREAMS)
@@ -81,6 +81,10 @@ def tile_plelayer_pb_t_kernel(tc, task_h, share_h, ews1, ebs1, ew1, eb1, gate_pr
             in_=ew1.rearrange("s (a q e) v x -> q s a (e v x)", a=4, q=P, e=2),
         )
 
+        warm = const.tile([P, 1], F32)
+        nc.vector.memset(warm[:], 0.0)
+        nc.scalar.activation(out=warm[:], in_=warm[:], func=ACT.Exp)
+
         gate = const.tile([P, T * ROWS, G], F32)
         nc.vector.tensor_tensor(
             out=gate[:].rearrange("p (t j) g -> p t j g", t=T),
@@ -90,7 +94,7 @@ def tile_plelayer_pb_t_kernel(tc, task_h, share_h, ews1, ebs1, ew1, eb1, gate_pr
         )
         gate_max = const.tile([P, T * ROWS], F32)
         nc.vector.tensor_reduce(out=gate_max[:], in_=gate[:], axis=AX.X, op=ALU.max)
-        nc.vector.tensor_tensor(
+        nc.gpsimd.tensor_tensor(
             out=gate[:],
             in0=gate[:],
             in1=gate_max[:].unsqueeze(2).to_broadcast([P, T * ROWS, G]),
@@ -158,33 +162,45 @@ def tile_plelayer_pb_t_kernel(tc, task_h, share_h, ews1, ebs1, ew1, eb1, gate_pr
             for j in range(J):
                 nc.tensor.transpose(nat_tiles[n][:, j, :], relu_tiles[n][:, j * P : (j + 1) * P], ident[:])
 
-        def weigh(n, t, half):
+        def weigh(n, t, half, dest):
             chunk = n // STREAMS
             rows = slice(t * ROWS + chunk * J, t * ROWS + (chunk + 1) * J)
             nc.vector.tensor_tensor(
-                out=prod_tiles[(chunk, t)][:, :, :, half * E : (half + 1) * E],
+                out=dest[:].rearrange("p (j v e) -> p j v e", j=J, v=V),
                 in0=nat_tiles[n][:].rearrange("p j (v e) -> p j v e", v=V),
                 in1=gate[:, rows, half * E : (half + 1) * E].unsqueeze(2).to_broadcast([P, J, V, E]),
                 op=ALU.mult,
             )
 
-        def gate_and_sum(n):
+        def gate_products(n):
             chunk, s = divmod(n, STREAMS)
             if s == 0:
                 for t in range(T):
-                    prod_tiles[(chunk, t)] = prod_pool.tile([P, J, V, G], F32, name="prod")
-                    weigh(n, t, 1)
+                    sum_tiles[(chunk, t)] = shared_pool.tile([P, J * C], F32, name="shared_prod")
+                    weigh(n, t, 1, sum_tiles[(chunk, t)])
             else:
-                t = s - 1
-                weigh(n, t, 0)
+                own_prod = mx_pool.tile([P, J * C], F32, name="own_prod")
+                weigh(n, s - 1, 0, own_prod)
+                both = sum_tiles[(chunk, s - 1)]
+                nc.gpsimd.tensor_tensor(out=both[:], in0=both[:], in1=own_prod[:], op=ALU.add)
+
+        def sum_experts(n):
+            chunk, s = divmod(n, STREAMS)
+            cols = slice(chunk * J * V, (chunk + 1) * J * V)
+            if s > 0:
                 nc.vector.tensor_reduce(
-                    out=out_sb[:, t, chunk * J * V : (chunk + 1) * J * V],
-                    in_=prod_tiles[(chunk, t)][:].rearrange("p j v g -> p (j v) g"),
+                    out=out_sb[:, s - 1, cols],
+                    in_=sum_tiles[(chunk, s - 1)][:].rearrange("p (r e) -> p r e", e=E),
                     axis=AX.X,
                     op=ALU.add,
                 )
             if s == T:
-                cols = slice(chunk * J * V, (chunk + 1) * J * V)
+                nc.gpsimd.tensor_tensor(
+                    out=out_sb[:, :, cols].rearrange("p t (j v) -> p t j v", j=J),
+                    in0=out_sb[:, :, cols].rearrange("p t (j v) -> p t j v", j=J),
+                    in1=gate_rsum[:, :, chunk * J : (chunk + 1) * J].unsqueeze(3).to_broadcast([P, T, J, V]),
+                    op=ALU.mult,
+                )
                 nc.sync.dma_start(out=out_rows[:, :, cols], in_=out_sb[:, :, cols])
 
         out_sb = const.tile([P, T, ROWS * V], F32)
@@ -197,17 +213,11 @@ def tile_plelayer_pb_t_kernel(tc, task_h, share_h, ews1, ebs1, ew1, eb1, gate_pr
         nc.vector.tensor_copy(out=bias_col[:], in_=bias_ps[:, 0, 0:STREAMS])
 
         nc.scalar.activation(out=gate[:], in_=gate[:], func=ACT.Exp)
-        gate_sum = const.tile([P, T * ROWS], F32)
-        nc.vector.tensor_reduce(out=gate_sum[:], in_=gate[:], axis=AX.X, op=ALU.add)
-        nc.vector.reciprocal(out=gate_sum[:], in_=gate_sum[:])
-        nc.vector.tensor_tensor(
-            out=gate[:],
-            in0=gate[:],
-            in1=gate_sum[:].unsqueeze(2).to_broadcast([P, T * ROWS, G]),
-            op=ALU.mult,
-        )
+        gate_rsum = const.tile([P, T, ROWS], F32)
+        nc.vector.tensor_reduce(out=gate_rsum[:].rearrange("p t j -> p (t j)"), in_=gate[:], axis=AX.X, op=ALU.add)
+        nc.vector.reciprocal(out=gate_rsum[:], in_=gate_rsum[:])
 
-        for step in range(1, UNITS + 3):
+        for step in range(1, UNITS + 4):
             if step + AHEAD - 1 < UNITS:
                 load(step + AHEAD - 1)
             if step - 1 < UNITS:
@@ -219,5 +229,7 @@ def tile_plelayer_pb_t_kernel(tc, task_h, share_h, ews1, ebs1, ew1, eb1, gate_pr
                 transpose_in(step)
             if 0 <= step - 2 < UNITS:
                 transpose_back(step - 2)
-            if 0 <= step - 3:
-                gate_and_sum(step - 3)
+            if 0 <= step - 3 < UNITS:
+                gate_products(step - 3)
+            if 0 <= step - 4:
+                sum_experts(step - 4)

@@ -116,11 +116,12 @@ def tile_plelayer_pb_t_kernel(tc, task_h, share_h, ews1, ebs1, ew1, eb1, gate_pr
                 in_=w_grouped[:, s].rearrange("q g c t -> q (g c t)"),
             )
 
-        def transpose_in(n):
+        def transpose_in(n, js):
             x_words = x_tiles[n][:].bitcast(F32)
-            grouped_tiles[n] = mx_pool.tile([P, PASSES * N * PACK], BF16, name="grouped", align_bytes=64)
+            if n not in grouped_tiles:
+                grouped_tiles[n] = mx_pool.tile([P, PASSES * N * PACK], BF16, name="grouped", align_bytes=64)
             grouped_words = grouped_tiles[n][:].bitcast(F32).rearrange("q (g c h) -> q g c h", g=PASSES, h=2)
-            for j in range(J):
+            for j in js:
                 xt = fwd_ps.tile([P, 4, P], F32, name="xt")
                 for a in range(4):
                     nc.tensor.transpose(xt[:, a, :], x_words[:, j * WORDS + a * P : j * WORDS + (a + 1) * P], ident[:])
@@ -138,7 +139,8 @@ def tile_plelayer_pb_t_kernel(tc, task_h, share_h, ews1, ebs1, ew1, eb1, gate_pr
 
         def expert_matmul(n):
             s = n % STREAMS
-            acc_tiles[n] = acc_ps.tile([P, N], F32, name="acc")
+            if n not in acc_tiles:
+                acc_tiles[n] = acc_ps.tile([P, N], F32, name="acc")
             for g in range(PASSES):
                 nc.tensor.matmul_mx(
                     out=acc_tiles[n][:],
@@ -205,7 +207,7 @@ def tile_plelayer_pb_t_kernel(tc, task_h, share_h, ews1, ebs1, ew1, eb1, gate_pr
 
         out_sb = const.tile([P, T, ROWS * V], F32)
 
-        transpose_in(0)
+        transpose_in(0, range(J))
 
         bias_ps = nat_ps.tile([P, J, C], F32, name="nat")
         nc.tensor.transpose(bias_ps[:, 0, :], bias_rows_f32[:], ident[:])
@@ -226,7 +228,11 @@ def tile_plelayer_pb_t_kernel(tc, task_h, share_h, ews1, ebs1, ew1, eb1, gate_pr
                 expert_matmul(step - 2)
                 bias_relu(step - 2)
             if step < UNITS:
-                transpose_in(step)
+                transpose_in(step, range(0, J // 2))
+            if 0 <= step - 2 < UNITS:
+                expert_matmul(step - 2)
+            if step < UNITS:
+                transpose_in(step, range(J // 2, J))
             if 0 <= step - 2 < UNITS:
                 transpose_back(step - 2)
             if 0 <= step - 3 < UNITS:

from contextlib import ExitStack

import concourse.mybir as mybir
from concourse.masks import make_identity

F32 = mybir.dt.float32
BF16 = mybir.dt.bfloat16
U32 = mybir.dt.uint32
U8 = mybir.dt.uint8
FP8X4 = mybir.dt.float8_e4m3fn_x4
ACT = mybir.ActivationFunctionType
ALU = mybir.AluOpType
AX = mybir.AxisListType

P = 128
T, B, U, V, E = 3, 4096, 1024, 16, 8
G = 2 * E
C = V * E
STREAMS = T + 1
PACK = 4
K_PASS = P * PACK
PASSES = U // K_PASS
ROWS = B // P
J = 4
N = J * P
CHUNKS = ROWS // J
UNITS = CHUNKS * STREAMS
WORDS = U // 2
AHEAD = 5

FLOPS = 2 * STREAMS * B * U * C


def tile_plelayer_pb_t_kernel(tc, task_h, share_h, ews1, ebs1, ew1, eb1, gate_pre1, gb1, out):
    nc = tc.nc
    stream_rows = [share_h.rearrange("(p j) u -> p (j u)", p=P)]
    stream_rows += [task_h[t].rearrange("(p j) u -> p (j u)", p=P) for t in range(T)]
    out_rows = out.rearrange("t (p j) v -> p t (j v)", p=P)

    with ExitStack() as ctx:
        const = ctx.enter_context(tc.tile_pool(name="const", bufs=1))
        x_pool = ctx.enter_context(tc.tile_pool(name="x", bufs=AHEAD + 1))
        mx_pool = ctx.enter_context(tc.tile_pool(name="mx", bufs=3))
        shared_pool = ctx.enter_context(tc.tile_pool(name="shared", bufs=2 * T))
        fwd_ps = ctx.enter_context(tc.psum_pool(name="fwd", bufs=4))
        acc_ps = ctx.enter_context(tc.psum_pool(name="acc", bufs=2))
        nat_ps = ctx.enter_context(tc.psum_pool(name="nat", bufs=2))
        ctx.enter_context(tc.manual_schedule())

        x_tiles, grouped_tiles, code_tiles, scale_tiles = {}, {}, {}, {}
        acc_tiles, relu_tiles, nat_tiles, sum_tiles = {}, {}, {}, {}

        def load(n):
            chunk, stream = divmod(n, STREAMS)
            x_tiles[n] = x_pool.tile([P, J * U], BF16, name="x_rows")
            nc.sync.dma_start(out=x_tiles[n][:], in_=stream_rows[stream][:, chunk * J * U : (chunk + 1) * J * U])

        ident = const.tile([P, P], F32)
        make_identity(nc, ident[:])
        bias_rows = const.tile([P, P], BF16)
        nc.vector.memset(bias_rows[:], 0.0)

        gate_raw = const.tile([P, T * ROWS * G], BF16)
        nc.sync.dma_start(
            out=gate_raw[:].rearrange("p (t r) -> p t r", t=T),
            in_=gate_pre1.rearrange("t (p j) g -> p t (j g)", p=P),
        )
        for n in range(AHEAD):
            load(n)
        gb_rep = const.tile([P, T * G], BF16)
        nc.scalar.dma_start(out=gb_rep[:], in_=gb1.rearrange("t g -> (t g)").partition_broadcast(P))
        nc.scalar.dma_start(out=bias_rows[0:1, :], in_=ebs1.rearrange("v x -> (v x)").unsqueeze(0))
        nc.scalar.dma_start(out=bias_rows[1:STREAMS, :], in_=eb1.rearrange("t v x -> t (v x)"))
        w_raw = const.tile([P, STREAMS, PASSES, PACK, C], BF16)
        nc.scalar.dma_start(
            out=w_raw[:, 0].rearrange("q g t c -> q (g t c)").rearrange("q (a r) -> q a r", a=4),
            in_=ews1.rearrange("(a q e) v x -> q a (e v x)", a=4, q=P, e=2),
        )
        nc.scalar.dma_start(
            out=w_raw[:, 1:STREAMS].rearrange("q s g t c -> q s (g t c)").rearrange("q s (a r) -> q s a r", a=4),
            in_=ew1.rearrange("s (a q e) v x -> q s a (e v x)", a=4, q=P, e=2),
        )

        warm = const.tile([P, 1], F32)
        nc.vector.memset(warm[:], 0.0)
        nc.scalar.activation(out=warm[:], in_=warm[:], func=ACT.Exp)

        gate = const.tile([P, T * ROWS, G], F32)
        nc.vector.tensor_tensor(
            out=gate[:].rearrange("p (t j) g -> p t j g", t=T),
            in0=gate_raw[:].rearrange("p (t j g) -> p t j g", t=T, j=ROWS),
            in1=gb_rep[:].rearrange("p (t g) -> p t g", t=T).unsqueeze(2).to_broadcast([P, T, ROWS, G]),
            op=ALU.add,
        )
        gate_max = const.tile([P, T * ROWS], F32)
        nc.vector.tensor_reduce(out=gate_max[:], in_=gate[:], axis=AX.X, op=ALU.max)
        nc.gpsimd.tensor_tensor(
            out=gate[:],
            in0=gate[:],
            in1=gate_max[:].unsqueeze(2).to_broadcast([P, T * ROWS, G]),
            op=ALU.subtract,
        )

        bias_rows_f32 = const.tile([P, P], F32)
        nc.vector.tensor_copy(out=bias_rows_f32[:], in_=bias_rows[:])

        w_grouped = const.tile([P, STREAMS, PASSES, C, PACK], BF16, align_bytes=64)
        w_codes = const.tile([P, STREAMS, PASSES, C], U32, align_bytes=64)
        w_scales = const.tile([P, STREAMS, PASSES, C], U8, align_bytes=64)
        for s in range(STREAMS):
            nc.vector.tensor_copy(out=w_grouped[:, s], in_=w_raw[:, s].rearrange("q g t c -> q g c t"))
        for s in range(STREAMS):
            nc.vector.quantize_mx(
                out=w_codes[:, s].rearrange("q g c -> q (g c)").bitcast(FP8X4),
                scales=w_scales[:, s].rearrange("q g c -> q (g c)"),
                in_=w_grouped[:, s].rearrange("q g c t -> q (g c t)"),
            )

        def transpose_in(n, js):
            x_words = x_tiles[n][:].bitcast(F32)
            if n not in grouped_tiles:
                grouped_tiles[n] = mx_pool.tile([P, PASSES * N * PACK], BF16, name="grouped", align_bytes=64)
            grouped_words = grouped_tiles[n][:].bitcast(F32).rearrange("q (g c h) -> q g c h", g=PASSES, h=2)
            for j in js:
                xt = fwd_ps.tile([P, 4, P], F32, name="xt")
                for a in range(4):
                    nc.tensor.transpose(xt[:, a, :], x_words[:, j * WORDS + a * P : j * WORDS + (a + 1) * P], ident[:])
                nc.scalar.copy(
                    out=grouped_words[:, :, j * P : (j + 1) * P, :],
                    in_=xt[:].rearrange("q (g h) r -> q g r h", g=PASSES),
                )

        def quantise(n):
            code_tiles[n] = mx_pool.tile([P, PASSES * N], U32, name="codes", align_bytes=64)
            scale_tiles[n] = mx_pool.tile([P, PASSES * N], U8, name="scales", align_bytes=64)
            nc.vector.quantize_mx(
                out=code_tiles[n][:].bitcast(FP8X4), scales=scale_tiles[n][:], in_=grouped_tiles[n][:]
            )

        def expert_matmul(n):
            s = n % STREAMS
            if n not in acc_tiles:
                acc_tiles[n] = acc_ps.tile([P, N], F32, name="acc")
            for g in range(PASSES):
                nc.tensor.matmul_mx(
                    out=acc_tiles[n][:],
                    lhsT=w_codes[:, s, g, :].bitcast(FP8X4),
                    lhsT_scale=w_scales[:, s, g, :],
                    rhs=code_tiles[n][:, g * N : (g + 1) * N].bitcast(FP8X4),
                    rhs_scale=scale_tiles[n][:, g * N : (g + 1) * N],
                    start=(g == 0),
                    stop=(g == PASSES - 1),
                )

        def bias_relu(n):
            s = n % STREAMS
            relu_tiles[n] = mx_pool.tile([P, N], F32, name="relu")
            nc.scalar.activation(
                out=relu_tiles[n][:], in_=acc_tiles[n][:], func=ACT.Relu, bias=bias_col[:, s : s + 1], scale=1.0
            )

        def transpose_back(n):
            nat_tiles[n] = nat_ps.tile([P, J, C], F32, name="nat")
            for j in range(J):
                nc.tensor.transpose(nat_tiles[n][:, j, :], relu_tiles[n][:, j * P : (j + 1) * P], ident[:])

        def weigh(n, t, half, dest):
            chunk = n // STREAMS
            rows = slice(t * ROWS + chunk * J, t * ROWS + (chunk + 1) * J)
            nc.vector.tensor_tensor(
                out=dest[:].rearrange("p (j v e) -> p j v e", j=J, v=V),
                in0=nat_tiles[n][:].rearrange("p j (v e) -> p j v e", v=V),
                in1=gate[:, rows, half * E : (half + 1) * E].unsqueeze(2).to_broadcast([P, J, V, E]),
                op=ALU.mult,
            )

        def gate_products(n):
            chunk, s = divmod(n, STREAMS)
            if s == 0:
                for t in range(T):
                    sum_tiles[(chunk, t)] = shared_pool.tile([P, J * C], F32, name="shared_prod")
                    weigh(n, t, 1, sum_tiles[(chunk, t)])
            else:
                own_prod = mx_pool.tile([P, J * C], F32, name="own_prod")
                weigh(n, s - 1, 0, own_prod)
                both = sum_tiles[(chunk, s - 1)]
                nc.gpsimd.tensor_tensor(out=both[:], in0=both[:], in1=own_prod[:], op=ALU.add)

        def sum_experts(n):
            chunk, s = divmod(n, STREAMS)
            cols = slice(chunk * J * V, (chunk + 1) * J * V)
            if s > 0:
                nc.vector.tensor_reduce(
                    out=out_sb[:, s - 1, cols],
                    in_=sum_tiles[(chunk, s - 1)][:].rearrange("p (r e) -> p r e", e=E),
                    axis=AX.X,
                    op=ALU.add,
                )
            if s == T:
                nc.gpsimd.tensor_tensor(
                    out=out_sb[:, :, cols].rearrange("p t (j v) -> p t j v", j=J),
                    in0=out_sb[:, :, cols].rearrange("p t (j v) -> p t j v", j=J),
                    in1=gate_rsum[:, :, chunk * J : (chunk + 1) * J].unsqueeze(3).to_broadcast([P, T, J, V]),
                    op=ALU.mult,
                )
                nc.sync.dma_start(out=out_rows[:, :, cols], in_=out_sb[:, :, cols])

        out_sb = const.tile([P, T, ROWS * V], F32)

        transpose_in(0, range(J))

        bias_ps = nat_ps.tile([P, J, C], F32, name="nat")
        nc.tensor.transpose(bias_ps[:, 0, :], bias_rows_f32[:], ident[:])
        bias_col = const.tile([P, STREAMS], F32)
        nc.vector.tensor_copy(out=bias_col[:], in_=bias_ps[:, 0, 0:STREAMS])

        nc.scalar.activation(out=gate[:], in_=gate[:], func=ACT.Exp)
        gate_rsum = const.tile([P, T, ROWS], F32)
        nc.vector.tensor_reduce(out=gate_rsum[:].rearrange("p t j -> p (t j)"), in_=gate[:], axis=AX.X, op=ALU.add)
        nc.vector.reciprocal(out=gate_rsum[:], in_=gate_rsum[:])

        for step in range(1, UNITS + 4):
            if step + AHEAD - 1 < UNITS:
                load(step + AHEAD - 1)
            if step - 1 < UNITS:
                quantise(step - 1)
            if 0 <= step - 2 < UNITS:
                expert_matmul(step - 2)
                bias_relu(step - 2)
            if step < UNITS:
                transpose_in(step, range(0, J // 2))
            if 0 <= step - 2 < UNITS:
                expert_matmul(step - 2)
            if step < UNITS:
                transpose_in(step, range(J // 2, J))
            if 0 <= step - 2 < UNITS:
                transpose_back(step - 2)
            if 0 <= step - 3 < UNITS:
                gate_products(step - 3)
            if 0 <= step - 4:
                sum_experts(step - 4)
